import numpy as np
import ml_dtypes


def mxq(x, axis, fmt="e4m3"):
    dtype, down = {"e4m3": (ml_dtypes.float8_e4m3fn, 7), "e5m2": (ml_dtypes.float8_e5m2, 14)}[fmt]
    v = np.moveaxis(np.asarray(x, np.float32).astype(ml_dtypes.bfloat16).astype(np.float64), axis, -1)
    blocks = v.reshape(v.shape[:-1] + (-1, 32))
    amax = np.abs(blocks).max(-1, keepdims=True)
    byte = np.maximum(np.where(amax > 0, np.frexp(amax)[1] - 1 + 127, 0) - down, 1)
    scale = np.exp2(byte - 127.0)
    codes = (blocks / scale).astype(np.float32).astype(dtype).astype(np.float64)
    return np.moveaxis((codes * scale).reshape(v.shape), -1, axis)


WIDE = False


def mx_kscale(k):
    if not WIDE:
        return np.ones(k)
    levels = np.array([10, -10, 5, -5, 0])
    if k % 512:
        return np.exp2(np.random.permutation(np.resize(levels, k // 32))).repeat(32)
    a = np.empty((k // 512, 16))
    for p in range(k // 512):
        a[p, :8] = np.random.permutation(np.resize(levels, 8))
        for g in range(8):
            far = levels[np.abs(levels - a[p, g]) >= 10]
            a[p, g + 8] = far[np.random.randint(len(far))]
    return np.exp2(a.ravel()).repeat(32)


BF16 = ml_dtypes.bfloat16


def bf(x):
    return np.asarray(x, np.float32).astype(BF16)


def f64(x):
    return np.asarray(x).astype(np.float64)


B, C, NP, P, HID = 16, 3, 8, 32, 512
IN_D = C * P * P
NTOK = NP * NP
SEQ = NTOK + 1
IMG = NP * P
T = B * NTOK


def positional_embedding(seq_len, dim):
    i = np.arange(seq_len)[:, None].astype(np.float64)
    j = np.arange(dim)[None, :].astype(np.float64)
    ang = i / np.power(100000.0, j / dim)
    return np.where(j % 2 == 0, np.sin(ang), np.cos(ang))


def to_patches(X):
    nb = X.shape[0]
    return X.reshape(nb, C, NP, P, NP, P).transpose(0, 2, 4, 1, 3, 5).reshape(nb * NTOK, IN_D)


def from_patches(patches):
    nb = patches.shape[0] // NTOK
    return patches.reshape(nb, NP, NP, C, P, P).transpose(0, 3, 1, 4, 2, 5).reshape(nb, C, IMG, IMG)


def setup_inputs():
    s = mx_kscale(T)
    u = mx_kscale(HID)
    sx = s.reshape(B, 1, NP, 1, NP, 1)
    sg = np.concatenate([np.ones((B, 1, 1)), s.reshape(B, NTOK, 1)], axis=1)
    bound = 2.0 / np.sqrt(IN_D)
    X = np.random.standard_normal((B, C, NP, P, NP, P)) * sx
    W = np.random.uniform(-bound, bound, (HID, IN_D)) / u[:, None]
    b = np.random.standard_normal(HID) * 0.3
    cls = np.random.uniform(0.0, 1.0, (1, HID))
    g = np.random.standard_normal((B, SEQ, HID)) * np.exp2(np.random.randint(-6, 1, (B, SEQ, 1))) * 4.0
    g = g / sg * u
    return {"X": bf(X.reshape(B, C, IMG, IMG)),
            "W": bf(W),
            "b": bf(b),
            "class_token": bf(cls),
            "pos_embed": bf(positional_embedding(SEQ, HID)),
            "grad_out": bf(g)}


def reference(X, W, b, class_token, pos_embed, grad_out):
    nb = X.shape[0]
    dz = f64(grad_out)[:, 1:, :] * f64(pos_embed)[None, 1:, :]
    dz = dz.reshape(nb * NTOK, HID)
    patches = to_patches(f64(X))
    dp = mxq(dz, 1, "e5m2") @ mxq(f64(W), 0, "e4m3")
    dW = mxq(dz, 0, "e5m2").T @ mxq(patches, 0, "e4m3")
    return from_patches(dp), dW

@@ -1,0 +1,263 @@
+from contextlib import ExitStack
+
+import concourse.mybir as mybir
+from concourse.masks import make_identity
+
+IMAGES, CHANNELS, GRID, PATCH, HID = 16, 3, 8, 32, 512
+TOKENS = GRID * GRID
+IN_D = CHANNELS * PATCH * PATCH
+SIDE = GRID * PATCH
+
+FLOPS = 2 * 2 * IMAGES * TOKENS * HID * IN_D
+BYTES = 2 * (
+    IMAGES * CHANNELS * SIDE * SIDE + HID * IN_D + TOKENS * HID + IMAGES * TOKENS * HID
+) + 4 * (IMAGES * CHANNELS * SIDE * SIDE + HID * IN_D)
+
+F32 = mybir.dt.float32
+BF16 = mybir.dt.bfloat16
+U32 = mybir.dt.uint32
+U8 = mybir.dt.uint8
+E4M3 = mybir.dt.float8_e4m3fn_x4
+E5M2 = mybir.dt.float8_e5m2_x4
+
+P = 128
+PACK = 4
+N_TILE = 512
+CHUNKS = 2 * CHANNELS
+
+
+def tile_myvit_v_kernel(tc, X, W, b, class_token, pos_embed, grad_out, out_0, out_1):
+    nc = tc.nc
+    with ExitStack() as ctx:
+        const = ctx.enter_context(tc.tile_pool(name="const", bufs=1))
+        xin = ctx.enter_context(tc.tile_pool(name="xin", bufs=6))
+        win = ctx.enter_context(tc.tile_pool(name="win", bufs=2))
+        work = ctx.enter_context(tc.tile_pool(name="work", bufs=4))
+        mid = ctx.enter_context(tc.tile_pool(name="mid", bufs=2))
+        wq = ctx.enter_context(tc.tile_pool(name="wq", bufs=3))
+        xq = ctx.enter_context(tc.tile_pool(name="xq", bufs=4))
+        st0 = ctx.enter_context(tc.tile_pool(name="st0", bufs=3))
+        st1 = ctx.enter_context(tc.tile_pool(name="st1", bufs=4))
+        acc_pool = ctx.enter_context(tc.psum_pool(name="acc", bufs=4))
+        tr_pool = ctx.enter_context(tc.psum_pool(name="tr", bufs=4))
+
+        pos = const.tile([P, HID], BF16, name="pos")
+        nc.vector.memset(pos[TOKENS:P, :], 0.0)
+        nc.sync.dma_start(out=pos[0:TOKENS, :], in_=pos_embed[1 : 1 + TOKENS, :])
+        grad = work.tile([P, GRID, HID], BF16, name="grad", tag="work", align_bytes=64)
+        for gy in range(GRID):
+            nc.sync.dma_start(
+                out=grad[:, gy, :], in_=grad_out[:, 1 + GRID * gy : 1 + GRID * (gy + 1), :]
+            )
+        w_rows = W.rearrange("(p j) w -> p j w", j=PACK)
+        w_raw, x_raw = [], []
+        for c in range(CHANNELS):
+            w_tile = win.tile([P, PACK, PATCH * PATCH], BF16, name="w_tile", align_bytes=64)
+            nc.sync.dma_start(
+                out=w_tile[:], in_=w_rows[:, :, c * PATCH * PATCH : (c + 1) * PATCH * PATCH]
+            )
+            w_raw.append(w_tile)
+            for g in range(2):
+                x_tile = xin.tile([P, IMAGES, SIDE], BF16, name="x_tile", align_bytes=64)
+                nc.sync.dma_start(
+                    out=x_tile[:],
+                    in_=X[:, c, g * P : (g + 1) * P, :].rearrange("n y x -> y n x"),
+                )
+                x_raw.append(x_tile)
+
+        ident = const.tile([P, P], BF16, name="ident")
+        make_identity(nc, ident[:])
+        ident_f = const.tile([P, P], F32, name="ident_f")
+        make_identity(nc, ident_f[:])
+        spread = const.tile([P, GRID, IMAGES, GRID], BF16, name="spread")
+        nc.vector.tensor_copy(
+            out=spread[:],
+            in_=ident[:, 0:TOKENS]
+            .rearrange("p (y x) -> p y x", x=GRID)
+            .unsqueeze(2)
+            .to_broadcast([P, GRID, IMAGES, GRID]),
+        )
+        perm_x = const.tile([P, PATCH, PACK], BF16, name="perm_x")
+        nc.vector.tensor_copy(out=perm_x[:], in_=ident[:].rearrange("p (t y) -> p y t", t=PACK))
+        perm_d = const.tile([P, GRID, IMAGES], F32, name="perm_d")
+        nc.vector.tensor_copy(
+            out=perm_d[:], in_=ident_f[:].rearrange("p (n x) -> p x n", x=GRID)
+        )
+
+        dz = work.tile([P, GRID, HID], BF16, name="dz", tag="work", align_bytes=64)
+        for a in range(GRID // 2):
+            bank = tr_pool.tile([P, 2, HID], BF16, name="pos_bank", tag="tr")
+            for e in range(2):
+                nc.tensor.matmul(
+                    out=bank[:, e, :],
+                    lhsT=spread[:, 2 * a + e, :, :].rearrange("p n x -> p (n x)"),
+                    rhs=pos[:],
+                    start=True,
+                    stop=True,
+                )
+            for e in range(2):
+                gy = 2 * a + e
+                nc.vector.tensor_tensor(
+                    out=dz[:, gy, :], in0=grad[:, gy, :], in1=bank[:, e, :], op=mybir.AluOpType.mult
+                )
+
+        dzf = work.tile([P, 8 * P, PACK], BF16, name="dzf", tag="work", align_bytes=64)
+        dzf_words = (
+            dzf[:].rearrange("p m t -> p (m t)").bitcast(F32).rearrange("p (r k) -> p r k", k=16)
+        )
+        for a in range(GRID // 2):
+            bank = tr_pool.tile([P, 4, P], F32, name="dz_bank", tag="tr")
+            for e in range(2):
+                words = dz[:, 2 * a + e, :].bitcast(F32)
+                for u in range(2):
+                    nc.tensor.transpose(
+                        bank[:, 2 * e + u, :],
+                        words[:, u : HID // 2 : 2],
+                        perm_d[:].rearrange("p x n -> p (x n)"),
+                    )
+            src = bank[:].rearrange("p k r -> p r k")
+            dst = dzf_words[:, :, 4 * a : 4 * a + 4]
+            if a % 2 == 0:
+                nc.vector.tensor_copy(out=dst, in_=src)
+            else:
+                nc.scalar.copy(out=dst, in_=src)
+        dzf_codes = const.tile([P, 8 * P], U32, name="dzf_codes", align_bytes=64)
+        dzf_scales = const.tile([P, 8 * P], U8, name="dzf_scales", align_bytes=64)
+        nc.vector.quantize_mx(
+            out=dzf_codes[:].bitcast(E5M2),
+            scales=dzf_scales[:],
+            in_=dzf[:].rearrange("p m t -> p (m t)"),
+        )
+
+        dzt_codes = const.tile([P, 2, HID], U32, name="dzt_codes", align_bytes=64)
+        dzt_scales = const.tile([P, 2, HID], U8, name="dzt_scales", align_bytes=64)
+
+        def tokens_grouped(g):
+            t = mid.tile([P, HID, PACK], BF16, name="dzt", align_bytes=64)
+            nc.vector.tensor_copy(
+                out=t[:], in_=dz[:, PACK * g : PACK * (g + 1), :].rearrange("p t f -> p f t")
+            )
+            return t
+
+        def tokens_quantized(g, t):
+            nc.vector.quantize_mx(
+                out=dzt_codes[:, g, :].bitcast(E5M2),
+                scales=dzt_scales[:, g, :],
+                in_=t[:].rearrange("p f t -> p (f t)"),
+            )
+
+        def weight_grouped(k, engine):
+            t = mid.tile([P, N_TILE, PACK], BF16, name="w_group", align_bytes=64)
+            src = w_raw[k // 2][:, :, (k % 2) * N_TILE : (k % 2 + 1) * N_TILE]
+            engine(out=t[:], in_=src.rearrange("p j w -> p w j"))
+            return t
+
+        def weight_quantized(t):
+            codes = wq.tile([P, N_TILE], U32, name="w_codes", align_bytes=64)
+            scales = wq.tile([P, N_TILE], U8, name="w_scales", align_bytes=64)
+            nc.vector.quantize_mx(
+                out=codes[:].bitcast(E4M3), scales=scales[:], in_=t[:].rearrange("p w j -> p (w j)")
+            )
+            return codes, scales
+
+        def image_transposes(k, x_group, j):
+            cols = x_raw[k][:].rearrange("p n x -> p (n x)")
+            bank = tr_pool.tile([P, PATCH, 8, PACK], BF16, name="x_bank", tag="tr")
+            for i in range(8):
+                nc.tensor.transpose(
+                    bank[:, :, i, :],
+                    cols[:, 8 * j + i : IMAGES * SIDE : PATCH],
+                    perm_x[:],
+                )
+            dst = x_group[:, :, 8 * j : 8 * (j + 1), :].rearrange("p y x t -> p y (x t)")
+            src = bank[:].rearrange("p y x t -> p y (x t)")
+            if j % 2 == 0:
+                nc.vector.tensor_copy(out=dst, in_=src)
+            else:
+                nc.scalar.copy(out=dst, in_=src)
+
+        def image_quantized(x_group):
+            codes = xq.tile([P, PATCH * PATCH], U32, name="x_codes", align_bytes=64)
+            scales = xq.tile([P, PATCH * PATCH], U8, name="x_scales", align_bytes=64)
+            nc.vector.quantize_mx(
+                out=codes[:].bitcast(E4M3),
+                scales=scales[:],
+                in_=x_group[:].rearrange("p y x t -> p (y x t)"),
+            )
+            return codes, scales
+
+        def image_gradient(stage, w, gx):
+            acc = acc_pool.tile([P, N_TILE], F32, name="acc", tag="acc")
+            cols = slice(gx * P, (gx + 1) * P)
+            nc.tensor.matmul_mx(
+                out=acc[:],
+                lhsT=dzf_codes[:, cols].bitcast(E5M2),
+                lhsT_scale=dzf_scales[:, cols],
+                rhs=w[0][:].bitcast(E4M3),
+                rhs_scale=w[1][:],
+                start=True,
+                stop=True,
+            )
+            nc.scalar.copy(
+                out=stage[:, :, gx, :], in_=acc[:].rearrange("p (y x) -> p y x", x=PATCH)
+            )
+
+        def weight_gradient(stage, xs, m, h, engine):
+            acc = acc_pool.tile([P, N_TILE], F32, name="acc1", tag="acc")
+            for g in range(2):
+                nc.tensor.matmul_mx(
+                    out=acc[:],
+                    lhsT=dzt_codes[:, g, m * P : (m + 1) * P].bitcast(E5M2),
+                    lhsT_scale=dzt_scales[:, g, m * P : (m + 1) * P],
+                    rhs=xs[g][0][:, h * N_TILE : (h + 1) * N_TILE].bitcast(E4M3),
+                    rhs_scale=xs[g][1][:, h * N_TILE : (h + 1) * N_TILE],
+                    start=(g == 0),
+                    stop=(g == 1),
+                )
+            engine(out=stage[:, h * N_TILE : (h + 1) * N_TILE], in_=acc[:])
+
+        def weight_gradient_rows(c, xs, m):
+            stage = st1.tile([P, PATCH * PATCH], F32, name="stage1", align_bytes=64)
+            weight_gradient(stage, xs, m, 0, nc.vector.tensor_copy)
+            weight_gradient(stage, xs, m, 1, nc.vector.tensor_copy if m % 2 else nc.scalar.copy)
+            nc.sync.dma_start(
+                out=out_1[m * P : (m + 1) * P, c * PATCH * PATCH : (c + 1) * PATCH * PATCH],
+                in_=stage[:],
+            )
+
+        w_next = weight_quantized(weight_grouped(0, nc.scalar.copy))
+        pending = [tokens_grouped(0), tokens_grouped(1)]
+        for g in range(2):
+            tokens_quantized(g, pending[g])
+
+        xs = []
+        for k in range(CHUNKS):
+            w = w_next
+            c, half = k // 2, k % 2
+            stage = st0.tile([P, PATCH // 2, GRID, PATCH], F32, name="stage0", align_bytes=64)
+            x_group = work.tile([P, PATCH, PATCH, PACK], BF16, name="x_group", tag="work", align_bytes=64)
+            if k + 1 < CHUNKS:
+                w_group = weight_grouped(k + 1, nc.vector.tensor_copy)
+            for gx in range(4):
+                image_gradient(stage, w, gx)
+            image_transposes(k, x_group, 0)
+            image_transposes(k, x_group, 1)
+            if k + 1 < CHUNKS:
+                w_next = weight_quantized(w_group)
+            for gx in range(4, 8):
+                image_gradient(stage, w, gx)
+            nc.sync.dma_start(
+                out=out_0[:, c, :, :].rearrange("n (g y) x -> n g (y x)", g=GRID)[
+                    :, :, half * (PATCH // 2) * SIDE : (half + 1) * (PATCH // 2) * SIDE
+                ],
+                in_=stage[:].rearrange("p y g x -> p (y g x)"),
+            )
+            if k >= 2:
+                weight_gradient_rows((k - 2) // 2, xs[2 * ((k - 2) // 2) : 2 * ((k - 2) // 2) + 2], 2 * (k % 2))
+            image_transposes(k, x_group, 2)
+            image_transposes(k, x_group, 3)
+            if k >= 2:
+                weight_gradient_rows((k - 2) // 2, xs[2 * ((k - 2) // 2) : 2 * ((k - 2) // 2) + 2], 2 * (k % 2) + 1)
+            xs.append(image_quantized(x_group))
+        for m in range(4):
+            weight_gradient_rows(2, xs[4:6], m)

@@ -30,9 +30,10 @@ def tile_myvit_v_kernel(tc, X, W, b, class_token, pos_embed, grad_out, out_0, ou
     nc = tc.nc
     with ExitStack() as ctx:
         const = ctx.enter_context(tc.tile_pool(name="const", bufs=1))
-        xin = ctx.enter_context(tc.tile_pool(name="xin", bufs=6))
+        xin = ctx.enter_context(tc.tile_pool(name="xin", bufs=5))
         win = ctx.enter_context(tc.tile_pool(name="win", bufs=2))
         work = ctx.enter_context(tc.tile_pool(name="work", bufs=4))
+        xcol = ctx.enter_context(tc.tile_pool(name="xcol", bufs=2))
         mid = ctx.enter_context(tc.tile_pool(name="mid", bufs=2))
         wq = ctx.enter_context(tc.tile_pool(name="wq", bufs=3))
         xq = ctx.enter_context(tc.tile_pool(name="xq", bufs=4))
@@ -160,21 +161,25 @@ def tile_myvit_v_kernel(tc, X, W, b, class_token, pos_embed, grad_out, out_0, ou
             )
             return codes, scales
 
-        def image_transposes(k, x_group, j):
-            cols = x_raw[k][:].rearrange("p n x -> p (n x)")
+        def image_columns(k):
+            t = xcol.tile([P, PATCH, P], BF16, name="x_cols", align_bytes=64)
+            nc.vector.tensor_copy(
+                out=t[:].rearrange("p (a i) r -> p a r i", i=4),
+                in_=x_raw[k][:].rearrange("p n (g a i) -> p a (n g) i", g=GRID, i=4),
+            )
+            return t
+
+        def image_transposes(x_cols, x_group, j):
             bank = tr_pool.tile([P, PATCH, 8, PACK], BF16, name="x_bank", tag="tr")
             for i in range(8):
                 nc.tensor.transpose(
                     bank[:, :, i, :],
-                    cols[:, 8 * j + i : IMAGES * SIDE : PATCH],
+                    x_cols[:, 8 * j + i, :],
                     perm_x[:],
                 )
             dst = x_group[:, :, 8 * j : 8 * (j + 1), :].rearrange("p y x t -> p y (x t)")
             src = bank[:].rearrange("p y x t -> p y (x t)")
-            if j % 2 == 0:
-                nc.vector.tensor_copy(out=dst, in_=src)
-            else:
-                nc.scalar.copy(out=dst, in_=src)
+            nc.scalar.copy(out=dst, in_=src)
 
         def image_quantized(x_group):
             codes = xq.tile([P, PATCH * PATCH], U32, name="x_codes", align_bytes=64)
@@ -236,12 +241,13 @@ def tile_myvit_v_kernel(tc, X, W, b, class_token, pos_embed, grad_out, out_0, ou
             c, half = k // 2, k % 2
             stage = st0.tile([P, PATCH // 2, GRID, PATCH], F32, name="stage0", align_bytes=64)
             x_group = work.tile([P, PATCH, PATCH, PACK], BF16, name="x_group", tag="work", align_bytes=64)
+            x_cols = image_columns(k)
             if k + 1 < CHUNKS:
                 w_group = weight_grouped(k + 1, nc.vector.tensor_copy)
             for gx in range(4):
                 image_gradient(stage, w, gx)
-            image_transposes(k, x_group, 0)
-            image_transposes(k, x_group, 1)
+            image_transposes(x_cols, x_group, 0)
+            image_transposes(x_cols, x_group, 1)
             if k + 1 < CHUNKS:
                 w_next = weight_quantized(w_group)
             for gx in range(4, 8):
@@ -254,8 +260,8 @@ def tile_myvit_v_kernel(tc, X, W, b, class_token, pos_embed, grad_out, out_0, ou
             )
             if k >= 2:
                 weight_gradient_rows((k - 2) // 2, xs[2 * ((k - 2) // 2) : 2 * ((k - 2) // 2) + 2], 2 * (k % 2))
-            image_transposes(k, x_group, 2)
-            image_transposes(k, x_group, 3)
+            image_transposes(x_cols, x_group, 2)
+            image_transposes(x_cols, x_group, 3)
             if k >= 2:
                 weight_gradient_rows((k - 2) // 2, xs[2 * ((k - 2) // 2) : 2 * ((k - 2) // 2) + 2], 2 * (k % 2) + 1)
             xs.append(image_quantized(x_group))

@@ -24,6 +24,9 @@ P = 128
 PACK = 4
 N_TILE = 512
 CHUNKS = 2 * CHANNELS
+BANK_PX = 8
+BANKS = CHANNELS * 2 * PATCH // BANK_PX
+SLOTS = 4 * CHUNKS
 
 
 def tile_myvit_v_kernel(tc, X, W, b, class_token, pos_embed, grad_out, out_0, out_1):
@@ -32,22 +35,22 @@ def tile_myvit_v_kernel(tc, X, W, b, class_token, pos_embed, grad_out, out_0, ou
         const = ctx.enter_context(tc.tile_pool(name="const", bufs=1))
         xin = ctx.enter_context(tc.tile_pool(name="xin", bufs=5))
         win = ctx.enter_context(tc.tile_pool(name="win", bufs=2))
-        work = ctx.enter_context(tc.tile_pool(name="work", bufs=4))
-        xcol = ctx.enter_context(tc.tile_pool(name="xcol", bufs=2))
+        xcol = ctx.enter_context(tc.tile_pool(name="xcol", bufs=5))
+        xgrp = ctx.enter_context(tc.tile_pool(name="xgrp", bufs=3))
         mid = ctx.enter_context(tc.tile_pool(name="mid", bufs=2))
         wq = ctx.enter_context(tc.tile_pool(name="wq", bufs=3))
-        xq = ctx.enter_context(tc.tile_pool(name="xq", bufs=4))
+        xq = ctx.enter_context(tc.tile_pool(name="xq", bufs=8))
         st0 = ctx.enter_context(tc.tile_pool(name="st0", bufs=3))
         st1 = ctx.enter_context(tc.tile_pool(name="st1", bufs=4))
-        acc_pool = ctx.enter_context(tc.psum_pool(name="acc", bufs=4))
-        tr_pool = ctx.enter_context(tc.psum_pool(name="tr", bufs=4))
+        acc_pool = ctx.enter_context(tc.psum_pool(name="acc", bufs=5))
+        tr_pool = ctx.enter_context(tc.psum_pool(name="tr", bufs=3))
+        ctx.enter_context(tc.manual_schedule())
 
         pos = const.tile([P, HID], BF16, name="pos")
-        nc.vector.memset(pos[TOKENS:P, :], 0.0)
         nc.sync.dma_start(out=pos[0:TOKENS, :], in_=pos_embed[1 : 1 + TOKENS, :])
-        grad = work.tile([P, GRID, HID], BF16, name="grad", tag="work", align_bytes=64)
+        grad = const.tile([P, GRID, HID], BF16, name="grad", align_bytes=64)
         for gy in range(GRID):
-            nc.sync.dma_start(
+            (nc.scalar if gy % 2 else nc.sync).dma_start(
                 out=grad[:, gy, :], in_=grad_out[:, 1 + GRID * gy : 1 + GRID * (gy + 1), :]
             )
         w_rows = W.rearrange("(p j) w -> p j w", j=PACK)
@@ -70,6 +73,7 @@ def tile_myvit_v_kernel(tc, X, W, b, class_token, pos_embed, grad_out, out_0, ou
         make_identity(nc, ident[:])
         ident_f = const.tile([P, P], F32, name="ident_f")
         make_identity(nc, ident_f[:])
+        nc.vector.memset(pos[TOKENS:P, :], 0.0)
         spread = const.tile([P, GRID, IMAGES, GRID], BF16, name="spread")
         nc.vector.tensor_copy(
             out=spread[:],
@@ -80,12 +84,8 @@ def tile_myvit_v_kernel(tc, X, W, b, class_token, pos_embed, grad_out, out_0, ou
         )
         perm_x = const.tile([P, PATCH, PACK], BF16, name="perm_x")
         nc.vector.tensor_copy(out=perm_x[:], in_=ident[:].rearrange("p (t y) -> p y t", t=PACK))
-        perm_d = const.tile([P, GRID, IMAGES], F32, name="perm_d")
-        nc.vector.tensor_copy(
-            out=perm_d[:], in_=ident_f[:].rearrange("p (n x) -> p x n", x=GRID)
-        )
 
-        dz = work.tile([P, GRID, HID], BF16, name="dz", tag="work", align_bytes=64)
+        dz = const.tile([P, GRID, HID], BF16, name="dz", align_bytes=64)
         for a in range(GRID // 2):
             bank = tr_pool.tile([P, 2, HID], BF16, name="pos_bank", tag="tr")
             for e in range(2):
@@ -102,41 +102,32 @@ def tile_myvit_v_kernel(tc, X, W, b, class_token, pos_embed, grad_out, out_0, ou
                     out=dz[:, gy, :], in0=grad[:, gy, :], in1=bank[:, e, :], op=mybir.AluOpType.mult
                 )
 
-        dzf = work.tile([P, 8 * P, PACK], BF16, name="dzf", tag="work", align_bytes=64)
-        dzf_words = (
-            dzf[:].rearrange("p m t -> p (m t)").bitcast(F32).rearrange("p (r k) -> p r k", k=16)
-        )
-        for a in range(GRID // 2):
-            bank = tr_pool.tile([P, 4, P], F32, name="dz_bank", tag="tr")
-            for e in range(2):
-                words = dz[:, 2 * a + e, :].bitcast(F32)
-                for u in range(2):
-                    nc.tensor.transpose(
-                        bank[:, 2 * e + u, :],
-                        words[:, u : HID // 2 : 2],
-                        perm_d[:].rearrange("p x n -> p (x n)"),
-                    )
-            src = bank[:].rearrange("p k r -> p r k")
-            dst = dzf_words[:, :, 4 * a : 4 * a + 4]
-            if a % 2 == 0:
-                nc.vector.tensor_copy(out=dst, in_=src)
-            else:
-                nc.scalar.copy(out=dst, in_=src)
-        dzf_codes = const.tile([P, 8 * P], U32, name="dzf_codes", align_bytes=64)
-        dzf_scales = const.tile([P, 8 * P], U8, name="dzf_scales", align_bytes=64)
-        nc.vector.quantize_mx(
-            out=dzf_codes[:].bitcast(E5M2),
-            scales=dzf_scales[:],
-            in_=dzf[:].rearrange("p m t -> p (m t)"),
-        )
+        def weight_grouped(k, q, t, engine):
+            src = w_raw[k // 2][:, :, (k % 2) * N_TILE + q * 256 : (k % 2) * N_TILE + (q + 1) * 256]
+            engine(
+                out=t[:, q * 256 : (q + 1) * 256, :].rearrange("p (c i) j -> p c j i", i=4),
+                in_=src.rearrange("p j (c i) -> p c j i", i=4),
+            )
+
+        def weight_tile():
+            return mid.tile([P, N_TILE, PACK], BF16, name="w_group", align_bytes=64)
+
+        def weight_quantized(t):
+            codes = wq.tile([P, N_TILE], U32, name="w_codes", align_bytes=64)
+            scales = wq.tile([P, N_TILE], U8, name="w_scales", align_bytes=64)
+            nc.vector.quantize_mx(
+                out=codes[:].bitcast(E4M3), scales=scales[:], in_=t[:].rearrange("p w j -> p (w j)")
+            )
+            return codes, scales
 
         dzt_codes = const.tile([P, 2, HID], U32, name="dzt_codes", align_bytes=64)
         dzt_scales = const.tile([P, 2, HID], U8, name="dzt_scales", align_bytes=64)
 
-        def tokens_grouped(g):
+        def tokens_grouped(g, engine):
             t = mid.tile([P, HID, PACK], BF16, name="dzt", align_bytes=64)
-            nc.vector.tensor_copy(
-                out=t[:], in_=dz[:, PACK * g : PACK * (g + 1), :].rearrange("p t f -> p f t")
+            engine(
+                out=t[:].rearrange("p (c i) t -> p c t i", i=4),
+                in_=dz[:, PACK * g : PACK * (g + 1), :].rearrange("p t (c i) -> p c t i", i=4),
             )
             return t
 
@@ -147,51 +138,82 @@ def tile_myvit_v_kernel(tc, X, W, b, class_token, pos_embed, grad_out, out_0, ou
                 in_=t[:].rearrange("p f t -> p (f t)"),
             )
 
-        def weight_grouped(k, engine):
-            t = mid.tile([P, N_TILE, PACK], BF16, name="w_group", align_bytes=64)
-            src = w_raw[k // 2][:, :, (k % 2) * N_TILE : (k % 2 + 1) * N_TILE]
-            engine(out=t[:], in_=src.rearrange("p j w -> p w j"))
-            return t
+        dzf = const.tile([P, 8 * P, PACK], BF16, name="dzf", align_bytes=64)
+        dzf_words = (
+            dzf[:]
+            .rearrange("p m t -> p (m t)")
+            .bitcast(F32)
+            .rearrange("p (x g n k) -> p x g n k", x=GRID, g=2, k=8)
+        )
+        for a in range(GRID // 2):
+            bank = tr_pool.tile([P, 4, P], F32, name="dz_bank", tag="tr")
+            for e in range(2):
+                words = dz[:, 2 * a + e, :].bitcast(F32)
+                for u in range(2):
+                    nc.tensor.transpose(
+                        bank[:, 2 * e + u, :], words[:, u : HID // 2 : 2], ident_f[:]
+                    )
+            src = bank[:].rearrange("p k (n x) -> p x n k", x=GRID)
+            dst = dzf_words[:, :, a // 2, :, 4 * (a % 2) : 4 * (a % 2) + 4]
+            if a % 2 == 0:
+                nc.scalar.copy(out=dst, in_=src)
+            else:
+                nc.vector.tensor_copy(out=dst, in_=src)
+        w_group = weight_tile()
+        weight_grouped(0, 0, w_group, nc.scalar.copy)
+        weight_grouped(0, 1, w_group, nc.scalar.copy)
+        dzf_codes = const.tile([P, 8 * P], U32, name="dzf_codes", align_bytes=64)
+        dzf_scales = const.tile([P, 8 * P], U8, name="dzf_scales", align_bytes=64)
+        dzt_0 = tokens_grouped(0, nc.vector.tensor_copy)
+        nc.vector.quantize_mx(
+            out=dzf_codes[:].bitcast(E5M2),
+            scales=dzf_scales[:],
+            in_=dzf[:].rearrange("p m t -> p (m t)"),
+        )
+        tokens_quantized(0, dzt_0)
+        w_next = weight_quantized(w_group)
 
-        def weight_quantized(t):
-            codes = wq.tile([P, N_TILE], U32, name="w_codes", align_bytes=64)
-            scales = wq.tile([P, N_TILE], U8, name="w_scales", align_bytes=64)
-            nc.vector.quantize_mx(
-                out=codes[:].bitcast(E4M3), scales=scales[:], in_=t[:].rearrange("p w j -> p (w j)")
-            )
-            return codes, scales
+        x_cols, x_groups, x_codes = {}, {}, {}
 
-        def image_columns(k):
-            t = xcol.tile([P, PATCH, P], BF16, name="x_cols", align_bytes=64)
+        def image_columns(i):
+            k, j = divmod(i, PATCH // BANK_PX)
+            t = xcol.tile([P, BANK_PX // 2, P, 2], BF16, name="x_col", align_bytes=64)
+            words = t[:].rearrange("p a r e -> p (a r e)").bitcast(F32)
+            raw = x_raw[k][:].rearrange("p n x -> p (n x)").bitcast(F32)
             nc.vector.tensor_copy(
-                out=t[:].rearrange("p (a i) r -> p a r i", i=4),
-                in_=x_raw[k][:].rearrange("p n (g a i) -> p a (n g) i", g=GRID, i=4),
+                out=words.rearrange("p (a i r) -> p a r i", a=2, i=2),
+                in_=raw.rearrange("p (r w i) -> p w r i", w=8, i=2)[:, 2 * j : 2 * j + 2],
             )
-            return t
+            x_cols[i] = t
 
-        def image_transposes(x_cols, x_group, j):
-            bank = tr_pool.tile([P, PATCH, 8, PACK], BF16, name="x_bank", tag="tr")
-            for i in range(8):
-                nc.tensor.transpose(
-                    bank[:, :, i, :],
-                    x_cols[:, 8 * j + i, :],
-                    perm_x[:],
+        def image_transposes(i):
+            bank = tr_pool.tile([P, PATCH, BANK_PX, PACK], BF16, name="x_bank", tag="tr")
+            for e in range(BANK_PX):
+                if i % 4 < 2:
+                    nc.tensor.matmul(
+                        out=bank[:, :, e, :], lhsT=x_cols[i][:, e // 2, :, e % 2], rhs=perm_x[:], start=True, stop=True
+                    )
+                else:
+                    nc.tensor.transpose(bank[:, :, e, :], x_cols[i][:, e // 2, :, e % 2], perm_x[:])
+            if i % 2 == 0:
+                x_groups[i // 2] = xgrp.tile(
+                    [P, 2, PATCH * BANK_PX * PACK], BF16, name="x_group", align_bytes=64
                 )
-            dst = x_group[:, :, 8 * j : 8 * (j + 1), :].rearrange("p y x t -> p y (x t)")
-            src = bank[:].rearrange("p y x t -> p y (x t)")
-            nc.scalar.copy(out=dst, in_=src)
+            (nc.vector.tensor_copy if i % 4 else nc.scalar.copy)(
+                out=x_groups[i // 2][:, i % 2, :], in_=bank[:].rearrange("p y x t -> p (y x t)")
+            )
 
-        def image_quantized(x_group):
-            codes = xq.tile([P, PATCH * PATCH], U32, name="x_codes", align_bytes=64)
-            scales = xq.tile([P, PATCH * PATCH], U8, name="x_scales", align_bytes=64)
+        def image_quantized(i):
+            codes = xq.tile([P, N_TILE], U32, name="x_codes", align_bytes=64)
+            scales = xq.tile([P, N_TILE], U8, name="x_scales", align_bytes=64)
             nc.vector.quantize_mx(
                 out=codes[:].bitcast(E4M3),
                 scales=scales[:],
-                in_=x_group[:].rearrange("p y x t -> p (y x t)"),
+                in_=x_groups[i][:].rearrange("p b f -> p (b f)"),
             )
-            return codes, scales
+            x_codes[i] = (codes, scales)
 
-        def image_gradient(stage, w, gx):
+        def image_gradient(stage, w, gx, engine):
             acc = acc_pool.tile([P, N_TILE], F32, name="acc", tag="acc")
             cols = slice(gx * P, (gx + 1) * P)
             nc.tensor.matmul_mx(
@@ -203,67 +225,110 @@ def tile_myvit_v_kernel(tc, X, W, b, class_token, pos_embed, grad_out, out_0, ou
                 start=True,
                 stop=True,
             )
-            nc.scalar.copy(
-                out=stage[:, :, gx, :], in_=acc[:].rearrange("p (y x) -> p y x", x=PATCH)
-            )
+            engine(out=stage[:, :, gx, :], in_=acc[:].rearrange("p (y x) -> p y x", x=PATCH))
 
-        def weight_gradient(stage, xs, m, h, engine):
+        stages = {}
+
+        def weight_gradient(c, m, h):
+            if h == 0:
+                stages[c, m] = st1.tile([P, PATCH, 2, 2, BANK_PX], F32, name="stage1", align_bytes=64)
             acc = acc_pool.tile([P, N_TILE], F32, name="acc1", tag="acc")
             for g in range(2):
+                codes, scales = x_codes[4 * c + 2 * g + h]
                 nc.tensor.matmul_mx(
                     out=acc[:],
                     lhsT=dzt_codes[:, g, m * P : (m + 1) * P].bitcast(E5M2),
                     lhsT_scale=dzt_scales[:, g, m * P : (m + 1) * P],
-                    rhs=xs[g][0][:, h * N_TILE : (h + 1) * N_TILE].bitcast(E4M3),
-                    rhs_scale=xs[g][1][:, h * N_TILE : (h + 1) * N_TILE],
+                    rhs=codes[:].bitcast(E4M3),
+                    rhs_scale=scales[:],
                     start=(g == 0),
                     stop=(g == 1),
                 )
-            engine(out=stage[:, h * N_TILE : (h + 1) * N_TILE], in_=acc[:])
+            return acc, c, m, h
 
-        def weight_gradient_rows(c, xs, m):
-            stage = st1.tile([P, PATCH * PATCH], F32, name="stage1", align_bytes=64)
-            weight_gradient(stage, xs, m, 0, nc.vector.tensor_copy)
-            weight_gradient(stage, xs, m, 1, nc.vector.tensor_copy if m % 2 else nc.scalar.copy)
-            nc.sync.dma_start(
-                out=out_1[m * P : (m + 1) * P, c * PATCH * PATCH : (c + 1) * PATCH * PATCH],
-                in_=stage[:],
+        def weight_gradient_out(acc, c, m, h, engine):
+            engine(
+                out=stages[c, m][:, :, h, :, :].rearrange("p y b x -> p b y x"),
+                in_=acc[:].rearrange("p (b y x) -> p b y x", b=2, x=BANK_PX),
             )
+            if h == 1:
+                nc.sync.dma_start(
+                    out=out_1[m * P : (m + 1) * P, c * PATCH * PATCH : (c + 1) * PATCH * PATCH],
+                    in_=stages[c, m][:].rearrange("p y h b x -> p (y h b x)"),
+                )
 
-        w_next = weight_quantized(weight_grouped(0, nc.scalar.copy))
-        pending = [tokens_grouped(0), tokens_grouped(1)]
-        for g in range(2):
-            tokens_quantized(g, pending[g])
-
-        xs = []
-        for k in range(CHUNKS):
-            w = w_next
-            c, half = k // 2, k % 2
-            stage = st0.tile([P, PATCH // 2, GRID, PATCH], F32, name="stage0", align_bytes=64)
-            x_group = work.tile([P, PATCH, PATCH, PACK], BF16, name="x_group", tag="work", align_bytes=64)
-            x_cols = image_columns(k)
-            if k + 1 < CHUNKS:
-                w_group = weight_grouped(k + 1, nc.vector.tensor_copy)
-            for gx in range(4):
-                image_gradient(stage, w, gx)
-            image_transposes(x_cols, x_group, 0)
-            image_transposes(x_cols, x_group, 1)
-            if k + 1 < CHUNKS:
-                w_next = weight_quantized(w_group)
-            for gx in range(4, 8):
-                image_gradient(stage, w, gx)
-            nc.sync.dma_start(
-                out=out_0[:, c, :, :].rearrange("n (g y) x -> n g (y x)", g=GRID)[
-                    :, :, half * (PATCH // 2) * SIDE : (half + 1) * (PATCH // 2) * SIDE
-                ],
-                in_=stage[:].rearrange("p y g x -> p (y g x)"),
-            )
-            if k >= 2:
-                weight_gradient_rows((k - 2) // 2, xs[2 * ((k - 2) // 2) : 2 * ((k - 2) // 2) + 2], 2 * (k % 2))
-            image_transposes(x_cols, x_group, 2)
-            image_transposes(x_cols, x_group, 3)
-            if k >= 2:
-                weight_gradient_rows((k - 2) // 2, xs[2 * ((k - 2) // 2) : 2 * ((k - 2) // 2) + 2], 2 * (k % 2) + 1)
-            xs.append(image_quantized(x_group))
-        for m in range(4):
-            weight_gradient_rows(2, xs[4:6], m)
+        lead = 3
+        x_slot = [i for i in range(BANKS)]
+        groups = []
+        for c in range(CHANNELS):
+            for m in range(4):
+                for h in range(2):
+                    groups.append((x_slot[8 * c + 7] + 2, c, m, h))
+        for i in range(lead):
+            image_columns(i)
+        ahead = lead
+        ws = {0: w_next}
+        w_groups = {}
+        todo_quant, todo_out = [], []
+        dzt_1 = None
+        count = 0
+        stores = []
+        for s in range(28):
+            k, r = divmod(s, 4)
+            if s < SLOTS:
+                if r == 0:
+                    stage = st0.tile([P, PATCH // 2, GRID, PATCH], F32, name="stage0", align_bytes=64)
+                for e in range(2):
+                    image_gradient(stage, ws[k], 2 * r + e, nc.scalar.copy)
+            for queue, out_ap, in_ap in stores:
+                queue.dma_start(out=out_ap, in_=in_ap)
+            stores = []
+            if s == 1:
+                dzt_1 = tokens_grouped(1, nc.vector.tensor_copy)
+            if s == 1 + 1:
+                tokens_quantized(1, dzt_1)
+            quantize = []
+            for i in range(BANKS):
+                if x_slot[i] == s:
+                    image_transposes(i)
+                    if ahead < BANKS:
+                        image_columns(ahead)
+                        ahead += 1
+                    if i % 2:
+                        quantize.append(i // 2)
+            if 0 <= k and k + 1 < CHUNKS and r in (0, 1):
+                if r == 0:
+                    w_groups[k + 1] = weight_tile()
+                weight_grouped(k + 1, r - 0, w_groups[k + 1], nc.vector.tensor_copy)
+            for args in todo_out:
+                weight_gradient_out(*args, nc.scalar.copy)
+                count += 1
+            todo_out = []
+            for n in range(2):
+                if groups and groups[0][0] <= s and (n == 0 or groups[0][0] + 4 <= s or s >= 20):
+                    slot, c, m, h = groups.pop(0)
+                    todo_out.append(weight_gradient(c, m, h))
+            if k + 1 < CHUNKS and r == 0 + 2:
+                ws[k + 1] = weight_quantized(w_groups[k + 1])
+            for i in todo_quant:
+                image_quantized(i)
+            todo_quant = quantize
+            if r == 3 and k < CHUNKS:
+                for g in range(2):
+                    stores.append(
+                        (
+                            nc.scalar if g else nc.sync,
+                            out_0[:, k // 2, g * P : (g + 1) * P, :].rearrange(
+                                "n (g y) x -> n g (y x)", g=PACK
+                            )[:, :, (k % 2) * (PATCH // 2) * SIDE : (k % 2 + 1) * (PATCH // 2) * SIDE],
+                            stage[g * 64 : (g + 1) * 64].rearrange("p y g x -> p (y g x)"),
+                        )
+                    )
+        for slot, c, m, h in groups:
+            todo_out.append(weight_gradient(c, m, h))
+            if len(todo_out) > 2:
+                weight_gradient_out(*todo_out.pop(0), nc.scalar.copy if count % 2 else nc.vector.tensor_copy)
+                count += 1
+        for args in todo_out:
+            weight_gradient_out(*args, nc.scalar.copy if count % 2 else nc.vector.tensor_copy)
+            count += 1

@@ -33,22 +33,22 @@ def tile_myvit_v_kernel(tc, X, W, b, class_token, pos_embed, grad_out, out_0, ou
     nc = tc.nc
     with ExitStack() as ctx:
         const = ctx.enter_context(tc.tile_pool(name="const", bufs=1))
-        xin = ctx.enter_context(tc.tile_pool(name="xin", bufs=5))
+        xin = ctx.enter_context(tc.tile_pool(name="xin", bufs=3))
         win = ctx.enter_context(tc.tile_pool(name="win", bufs=2))
         xcol = ctx.enter_context(tc.tile_pool(name="xcol", bufs=5))
-        xgrp = ctx.enter_context(tc.tile_pool(name="xgrp", bufs=3))
+        work = ctx.enter_context(tc.tile_pool(name="work", bufs=3))
         mid = ctx.enter_context(tc.tile_pool(name="mid", bufs=2))
         wq = ctx.enter_context(tc.tile_pool(name="wq", bufs=3))
-        xq = ctx.enter_context(tc.tile_pool(name="xq", bufs=8))
+        xq = ctx.enter_context(tc.tile_pool(name="xq", bufs=6))
         st0 = ctx.enter_context(tc.tile_pool(name="st0", bufs=3))
-        st1 = ctx.enter_context(tc.tile_pool(name="st1", bufs=4))
+        st1 = ctx.enter_context(tc.tile_pool(name="st1", bufs=5))
         acc_pool = ctx.enter_context(tc.psum_pool(name="acc", bufs=5))
         tr_pool = ctx.enter_context(tc.psum_pool(name="tr", bufs=3))
         ctx.enter_context(tc.manual_schedule())
 
         pos = const.tile([P, HID], BF16, name="pos")
         nc.sync.dma_start(out=pos[0:TOKENS, :], in_=pos_embed[1 : 1 + TOKENS, :])
-        grad = const.tile([P, GRID, HID], BF16, name="grad", align_bytes=64)
+        grad = work.tile([P, GRID, HID], BF16, name="grad", tag="work", align_bytes=64)
         for gy in range(GRID):
             (nc.scalar if gy % 2 else nc.sync).dma_start(
                 out=grad[:, gy, :], in_=grad_out[:, 1 + GRID * gy : 1 + GRID * (gy + 1), :]
@@ -61,13 +61,11 @@ def tile_myvit_v_kernel(tc, X, W, b, class_token, pos_embed, grad_out, out_0, ou
                 out=w_tile[:], in_=w_rows[:, :, c * PATCH * PATCH : (c + 1) * PATCH * PATCH]
             )
             w_raw.append(w_tile)
-            for g in range(2):
-                x_tile = xin.tile([P, IMAGES, SIDE], BF16, name="x_tile", align_bytes=64)
-                nc.sync.dma_start(
-                    out=x_tile[:],
-                    in_=X[:, c, g * P : (g + 1) * P, :].rearrange("n y x -> y n x"),
-                )
-                x_raw.append(x_tile)
+            x_tile = xin.tile([P, IMAGES, 2 * SIDE], BF16, name="x_tile", align_bytes=64)
+            nc.sync.dma_start(
+                out=x_tile[:], in_=X[:, c, :, :].rearrange("n (y l) x -> y n (l x)", l=2)
+            )
+            x_raw.append(x_tile)
 
         ident = const.tile([P, P], BF16, name="ident")
         make_identity(nc, ident[:])
@@ -82,10 +80,12 @@ def tile_myvit_v_kernel(tc, X, W, b, class_token, pos_embed, grad_out, out_0, ou
             .unsqueeze(2)
             .to_broadcast([P, GRID, IMAGES, GRID]),
         )
-        perm_x = const.tile([P, PATCH, PACK], BF16, name="perm_x")
-        nc.vector.tensor_copy(out=perm_x[:], in_=ident[:].rearrange("p (t y) -> p y t", t=PACK))
+        perm_x = const.tile([P, 2, PATCH // 2, PACK], BF16, name="perm_x")
+        nc.vector.tensor_copy(
+            out=perm_x[:], in_=ident[:].rearrange("p (g t y) -> p g y t", g=2, t=PACK)
+        )
 
-        dz = const.tile([P, GRID, HID], BF16, name="dz", align_bytes=64)
+        dz = work.tile([P, GRID, HID], BF16, name="dz", tag="work", align_bytes=64)
         for a in range(GRID // 2):
             bank = tr_pool.tile([P, 2, HID], BF16, name="pos_bank", tag="tr")
             for e in range(2):
@@ -138,7 +138,7 @@ def tile_myvit_v_kernel(tc, X, W, b, class_token, pos_embed, grad_out, out_0, ou
                 in_=t[:].rearrange("p f t -> p (f t)"),
             )
 
-        dzf = const.tile([P, 8 * P, PACK], BF16, name="dzf", align_bytes=64)
+        dzf = work.tile([P, 8 * P, PACK], BF16, name="dzf", tag="work", align_bytes=64)
         dzf_words = (
             dzf[:]
             .rearrange("p m t -> p (m t)")
@@ -176,40 +176,51 @@ def tile_myvit_v_kernel(tc, X, W, b, class_token, pos_embed, grad_out, out_0, ou
         x_cols, x_groups, x_codes = {}, {}, {}
 
         def image_columns(i):
-            k, j = divmod(i, PATCH // BANK_PX)
+            unit, j = divmod(i, 4)
+            c, l = divmod(unit, 2)
             t = xcol.tile([P, BANK_PX // 2, P, 2], BF16, name="x_col", align_bytes=64)
-            words = t[:].rearrange("p a r e -> p (a r e)").bitcast(F32)
-            raw = x_raw[k][:].rearrange("p n x -> p (n x)").bitcast(F32)
-            nc.vector.tensor_copy(
-                out=words.rearrange("p (a i r) -> p a r i", a=2, i=2),
-                in_=raw.rearrange("p (r w i) -> p w r i", w=8, i=2)[:, 2 * j : 2 * j + 2],
-            )
+            words = t[:].rearrange("p w r e -> p (w r e)").bitcast(F32)
+            raw = x_raw[c][:].rearrange("p n f -> p (n f)").bitcast(F32)
+            for a in range(2):
+                nc.vector.tensor_copy(
+                    out=words.rearrange("p (a i n x) -> p a n x i", a=2, i=2, x=GRID)[:, a],
+                    in_=raw.rearrange("p (n l x w i) -> p l w n x i", l=2, x=GRID, w=8, i=2)[
+                        :, l, 2 * j + a
+                    ],
+                )
             x_cols[i] = t
 
         def image_transposes(i):
-            bank = tr_pool.tile([P, PATCH, BANK_PX, PACK], BF16, name="x_bank", tag="tr")
+            bank = tr_pool.tile([P, 2, PATCH // 2, BANK_PX, PACK], BF16, name="x_bank", tag="tr")
             for e in range(BANK_PX):
                 if i % 4 < 2:
                     nc.tensor.matmul(
-                        out=bank[:, :, e, :], lhsT=x_cols[i][:, e // 2, :, e % 2], rhs=perm_x[:], start=True, stop=True
+                        out=bank[:, :, :, e, :],
+                        lhsT=x_cols[i][:, e // 2, :, e % 2],
+                        rhs=perm_x[:],
+                        start=True,
+                        stop=True,
                     )
                 else:
-                    nc.tensor.transpose(bank[:, :, e, :], x_cols[i][:, e // 2, :, e % 2], perm_x[:])
-            if i % 2 == 0:
-                x_groups[i // 2] = xgrp.tile(
-                    [P, 2, PATCH * BANK_PX * PACK], BF16, name="x_group", align_bytes=64
+                    nc.tensor.transpose(
+                        bank[:, :, :, e, :], x_cols[i][:, e // 2, :, e % 2], perm_x[:]
+                    )
+            if i % 4 == 0:
+                x_groups[i // 4] = work.tile(
+                    [P, 2, 4, 16 * BANK_PX * PACK], BF16, name="x_group", tag="work", align_bytes=64
                 )
-            (nc.vector.tensor_copy if i % 4 else nc.scalar.copy)(
-                out=x_groups[i // 2][:, i % 2, :], in_=bank[:].rearrange("p y x t -> p (y x t)")
+            (nc.vector.tensor_copy if i % 3 else nc.scalar.copy)(
+                out=x_groups[i // 4][:, :, i % 4, :],
+                in_=bank[:].rearrange("p g y x t -> p g (y x t)"),
             )
 
         def image_quantized(i):
-            codes = xq.tile([P, N_TILE], U32, name="x_codes", align_bytes=64)
-            scales = xq.tile([P, N_TILE], U8, name="x_scales", align_bytes=64)
+            codes = xq.tile([P, 2, N_TILE], U32, name="x_codes", align_bytes=64)
+            scales = xq.tile([P, 2, N_TILE], U8, name="x_scales", align_bytes=64)
             nc.vector.quantize_mx(
-                out=codes[:].bitcast(E4M3),
-                scales=scales[:],
-                in_=x_groups[i][:].rearrange("p b f -> p (b f)"),
+                out=codes[:].rearrange("p g n -> p (g n)").bitcast(E4M3),
+                scales=scales[:].rearrange("p g n -> p (g n)"),
+                in_=x_groups[i][:].rearrange("p g j f -> p (g j f)"),
             )
             x_codes[i] = (codes, scales)
 
@@ -230,17 +241,17 @@ def tile_myvit_v_kernel(tc, X, W, b, class_token, pos_embed, grad_out, out_0, ou
         stages = {}
 
         def weight_gradient(c, m, h):
+            codes, scales = x_codes[2 * c + h]
             if h == 0:
-                stages[c, m] = st1.tile([P, PATCH, 2, 2, BANK_PX], F32, name="stage1", align_bytes=64)
+                stages[c, m] = st1.tile([P, PATCH // 2, 2, 4, BANK_PX], F32, name="stage1", align_bytes=64)
             acc = acc_pool.tile([P, N_TILE], F32, name="acc1", tag="acc")
             for g in range(2):
-                codes, scales = x_codes[4 * c + 2 * g + h]
                 nc.tensor.matmul_mx(
                     out=acc[:],
                     lhsT=dzt_codes[:, g, m * P : (m + 1) * P].bitcast(E5M2),
                     lhsT_scale=dzt_scales[:, g, m * P : (m + 1) * P],
-                    rhs=codes[:].bitcast(E4M3),
-                    rhs_scale=scales[:],
+                    rhs=codes[:, g, :].bitcast(E4M3),
+                    rhs_scale=scales[:, g, :],
                     start=(g == 0),
                     stop=(g == 1),
                 )
@@ -248,17 +259,17 @@ def tile_myvit_v_kernel(tc, X, W, b, class_token, pos_embed, grad_out, out_0, ou
 
         def weight_gradient_out(acc, c, m, h, engine):
             engine(
-                out=stages[c, m][:, :, h, :, :].rearrange("p y b x -> p b y x"),
-                in_=acc[:].rearrange("p (b y x) -> p b y x", b=2, x=BANK_PX),
+                out=stages[c, m][:, :, h, :, :].rearrange("p y j x -> p j y x"),
+                in_=acc[:].rearrange("p (j y x) -> p j y x", j=4, x=BANK_PX),
             )
             if h == 1:
                 nc.sync.dma_start(
                     out=out_1[m * P : (m + 1) * P, c * PATCH * PATCH : (c + 1) * PATCH * PATCH],
-                    in_=stages[c, m][:].rearrange("p y h b x -> p (y h b x)"),
+                    in_=stages[c, m][:].rearrange("p y l j x -> p (y l j x)"),
                 )
 
         lead = 3
-        x_slot = [i for i in range(BANKS)]
+        x_slot = [i * 6 // 5 for i in range(BANKS)]
         groups = []
         for c in range(CHANNELS):
             for m in range(4):
@@ -273,7 +284,7 @@ def tile_myvit_v_kernel(tc, X, W, b, class_token, pos_embed, grad_out, out_0, ou
         dzt_1 = None
         count = 0
         stores = []
-        for s in range(28):
+        for s in range(36):
             k, r = divmod(s, 4)
             if s < SLOTS:
                 if r == 0:
@@ -294,18 +305,18 @@ def tile_myvit_v_kernel(tc, X, W, b, class_token, pos_embed, grad_out, out_0, ou
                     if ahead < BANKS:
                         image_columns(ahead)
                         ahead += 1
-                    if i % 2:
-                        quantize.append(i // 2)
+                    if i % 4 == 3:
+                        quantize.append(i // 4)
             if 0 <= k and k + 1 < CHUNKS and r in (0, 1):
                 if r == 0:
                     w_groups[k + 1] = weight_tile()
                 weight_grouped(k + 1, r - 0, w_groups[k + 1], nc.vector.tensor_copy)
             for args in todo_out:
-                weight_gradient_out(*args, nc.scalar.copy)
+                weight_gradient_out(*args, nc.scalar.copy if count % 2 else nc.vector.tensor_copy)
                 count += 1
             todo_out = []
             for n in range(2):
-                if groups and groups[0][0] <= s and (n == 0 or groups[0][0] + 4 <= s or s >= 20):
+                if groups and groups[0][0] <= s and s >= 24 and (n == 0 or groups[0][0] + 4 <= s or s >= 24):
                     slot, c, m, h = groups.pop(0)
                     todo_out.append(weight_gradient(c, m, h))
             if k + 1 < CHUNKS and r == 0 + 2:
@@ -314,16 +325,20 @@ def tile_myvit_v_kernel(tc, X, W, b, class_token, pos_embed, grad_out, out_0, ou
                 image_quantized(i)
             todo_quant = quantize
             if r == 3 and k < CHUNKS:
-                for g in range(2):
-                    stores.append(
-                        (
-                            nc.scalar if g else nc.sync,
-                            out_0[:, k // 2, g * P : (g + 1) * P, :].rearrange(
-                                "n (g y) x -> n g (y x)", g=PACK
-                            )[:, :, (k % 2) * (PATCH // 2) * SIDE : (k % 2 + 1) * (PATCH // 2) * SIDE],
-                            stage[g * 64 : (g + 1) * 64].rearrange("p y g x -> p (y g x)"),
+                y0 = (k % 2) * (PATCH // 2)
+                for n0 in (0, IMAGES // 2):
+                    for g in range(2):
+                        stores.append(
+                            (
+                                nc.gpsimd,
+                                out_0[n0 : n0 + 8, k // 2, g * P : (g + 1) * P, :].rearrange(
+                                    "n (g y) x -> n g (y x)", g=PACK
+                                )[:, :, y0 * SIDE : (y0 + PATCH // 2) * SIDE],
+                                stage[64 * g + 4 * n0 : 64 * g + 4 * n0 + 32].rearrange(
+                                    "p y g x -> p (y g x)"
+                                ),
+                            )
                         )
-                    )
         for slot, c, m, h in groups:
             todo_out.append(weight_gradient(c, m, h))
             if len(todo_out) > 2:

@@ -173,7 +173,7 @@ def tile_myvit_v_kernel(tc, X, W, b, class_token, pos_embed, grad_out, out_0, ou
         tokens_quantized(0, dzt_0)
         w_next = weight_quantized(w_group)
 
-        x_cols, x_groups, x_codes = {}, {}, {}
+        x_cols, x_banks, x_groups, x_codes = {}, {}, {}, {}
 
         def image_columns(i):
             unit, j = divmod(i, 4)
@@ -193,7 +193,7 @@ def tile_myvit_v_kernel(tc, X, W, b, class_token, pos_embed, grad_out, out_0, ou
         def image_transposes(i):
             bank = tr_pool.tile([P, 2, PATCH // 2, BANK_PX, PACK], BF16, name="x_bank", tag="tr")
             for e in range(BANK_PX):
-                if i % 4 < 2:
+                if i % 8 in (0, 1, 2, 4, 5):
                     nc.tensor.matmul(
                         out=bank[:, :, :, e, :],
                         lhsT=x_cols[i][:, e // 2, :, e % 2],
@@ -205,13 +205,16 @@ def tile_myvit_v_kernel(tc, X, W, b, class_token, pos_embed, grad_out, out_0, ou
                     nc.tensor.transpose(
                         bank[:, :, :, e, :], x_cols[i][:, e // 2, :, e % 2], perm_x[:]
                     )
+            x_banks[i] = bank
+
+        def image_grouped(i, engine):
             if i % 4 == 0:
                 x_groups[i // 4] = work.tile(
                     [P, 2, 4, 16 * BANK_PX * PACK], BF16, name="x_group", tag="work", align_bytes=64
                 )
-            (nc.vector.tensor_copy if i % 3 else nc.scalar.copy)(
+            engine(
                 out=x_groups[i // 4][:, :, i % 4, :],
-                in_=bank[:].rearrange("p g y x t -> p g (y x t)"),
+                in_=x_banks[i][:].rearrange("p g y x t -> p g (y x t)"),
             )
 
         def image_quantized(i):
@@ -268,69 +271,81 @@ def tile_myvit_v_kernel(tc, X, W, b, class_token, pos_embed, grad_out, out_0, ou
                     in_=stages[c, m][:].rearrange("p y l j x -> p (y l j x)"),
                 )
 
-        lead = 3
         x_slot = [i * 6 // 5 for i in range(BANKS)]
-        groups = []
-        for c in range(CHANNELS):
-            for m in range(4):
-                for h in range(2):
-                    groups.append((x_slot[8 * c + 7] + 2, c, m, h))
-        for i in range(lead):
+        groups = [(x_slot[8 * c + 7] + 3, c, m, h) for c in range(CHANNELS) for m in range(4) for h in range(2)]
+        v, a = nc.vector.tensor_copy, nc.scalar.copy
+        for i in range(3):
             image_columns(i)
-        ahead = lead
+        ahead = 3
         ws = {0: w_next}
         w_groups = {}
-        todo_quant, todo_out = [], []
+        banks, quants, outs, stores = [], [], [], []
         dzt_1 = None
         count = 0
-        stores = []
-        for s in range(36):
+
+        def weight_group_step(s):
+            kw, q = divmod(s + 4, 4)
+            if 1 <= kw < CHUNKS and q < 2:
+                if q == 0:
+                    w_groups[kw] = weight_tile()
+                weight_grouped(kw, q, w_groups[kw], v)
+
+        def weight_quantize_step(s):
+            kw, q = divmod(s + 4, 4)
+            if 1 <= kw < CHUNKS and q == 2:
+                ws[kw] = weight_quantized(w_groups[kw])
+
+        for s in range(4 - 4, 0):
+            weight_group_step(s)
+            weight_quantize_step(s)
+        s = 0
+        while s < SLOTS or groups or outs or banks or quants or stores:
             k, r = divmod(s, 4)
             if s < SLOTS:
                 if r == 0:
                     stage = st0.tile([P, PATCH // 2, GRID, PATCH], F32, name="stage0", align_bytes=64)
                 for e in range(2):
-                    image_gradient(stage, ws[k], 2 * r + e, nc.scalar.copy)
-            for queue, out_ap, in_ap in stores:
-                queue.dma_start(out=out_ap, in_=in_ap)
+                    image_gradient(stage, ws[k], 2 * r + e, a)
+            for out_ap, in_ap in stores:
+                nc.gpsimd.dma_start(out=out_ap, in_=in_ap)
             stores = []
             if s == 1:
-                dzt_1 = tokens_grouped(1, nc.vector.tensor_copy)
+                dzt_1 = tokens_grouped(1, v)
             if s == 1 + 1:
                 tokens_quantized(1, dzt_1)
-            quantize = []
+            weight_group_step(s)
+            new_banks = []
             for i in range(BANKS):
                 if x_slot[i] == s:
                     image_transposes(i)
+                    new_banks.append(i)
                     if ahead < BANKS:
                         image_columns(ahead)
                         ahead += 1
-                    if i % 4 == 3:
-                        quantize.append(i // 4)
-            if 0 <= k and k + 1 < CHUNKS and r in (0, 1):
-                if r == 0:
-                    w_groups[k + 1] = weight_tile()
-                weight_grouped(k + 1, r - 0, w_groups[k + 1], nc.vector.tensor_copy)
-            for args in todo_out:
-                weight_gradient_out(*args, nc.scalar.copy if count % 2 else nc.vector.tensor_copy)
+            weight_quantize_step(s)
+            new_quants = []
+            for i in banks:
+                image_grouped(i, v if i % 4 == 3 else a)
+                if i % 4 == 3:
+                    new_quants.append(i // 4)
+            banks = new_banks
+            for args in outs:
+                weight_gradient_out(*args, a if args[1] == 2 and (args[2] + args[3]) % 2 else v)
                 count += 1
-            todo_out = []
-            for n in range(2):
-                if groups and groups[0][0] <= s and s >= 24 and (n == 0 or groups[0][0] + 4 <= s or s >= 24):
+            outs = []
+            for n in range(3):
+                if groups and groups[0][0] <= s and (n == 0 or s >= 20) and (s >= 8):
                     slot, c, m, h = groups.pop(0)
-                    todo_out.append(weight_gradient(c, m, h))
-            if k + 1 < CHUNKS and r == 0 + 2:
-                ws[k + 1] = weight_quantized(w_groups[k + 1])
-            for i in todo_quant:
+                    outs.append(weight_gradient(c, m, h))
+            for i in quants:
                 image_quantized(i)
-            todo_quant = quantize
-            if r == 3 and k < CHUNKS:
+            quants = new_quants
+            if s < SLOTS and r == 3:
                 y0 = (k % 2) * (PATCH // 2)
                 for n0 in (0, IMAGES // 2):
                     for g in range(2):
                         stores.append(
                             (
-                                nc.gpsimd,
                                 out_0[n0 : n0 + 8, k // 2, g * P : (g + 1) * P, :].rearrange(
                                     "n (g y) x -> n g (y x)", g=PACK
                                 )[:, :, y0 * SIDE : (y0 + PATCH // 2) * SIDE],
@@ -339,11 +354,4 @@ def tile_myvit_v_kernel(tc, X, W, b, class_token, pos_embed, grad_out, out_0, ou
                                 ),
                             )
                         )
-        for slot, c, m, h in groups:
-            todo_out.append(weight_gradient(c, m, h))
-            if len(todo_out) > 2:
-                weight_gradient_out(*todo_out.pop(0), nc.scalar.copy if count % 2 else nc.vector.tensor_copy)
-                count += 1
-        for args in todo_out:
-            weight_gradient_out(*args, nc.scalar.copy if count % 2 else nc.vector.tensor_copy)
-            count += 1
+            s += 1

from contextlib import ExitStack

import concourse.mybir as mybir
from concourse.masks import make_identity

IMAGES, CHANNELS, GRID, PATCH, HID = 16, 3, 8, 32, 512
TOKENS = GRID * GRID
IN_D = CHANNELS * PATCH * PATCH
SIDE = GRID * PATCH

FLOPS = 2 * 2 * IMAGES * TOKENS * HID * IN_D
BYTES = 2 * (
    IMAGES * CHANNELS * SIDE * SIDE + HID * IN_D + TOKENS * HID + IMAGES * TOKENS * HID
) + 4 * (IMAGES * CHANNELS * SIDE * SIDE + HID * IN_D)

F32 = mybir.dt.float32
BF16 = mybir.dt.bfloat16
U32 = mybir.dt.uint32
U8 = mybir.dt.uint8
E4M3 = mybir.dt.float8_e4m3fn_x4
E5M2 = mybir.dt.float8_e5m2_x4

P = 128
PACK = 4
N_TILE = 512
CHUNKS = 2 * CHANNELS
BANK_PX = 8
BANKS = CHANNELS * 2 * PATCH // BANK_PX
SLOTS = 4 * CHUNKS


def tile_myvit_v_kernel(tc, X, W, b, class_token, pos_embed, grad_out, out_0, out_1):
    nc = tc.nc
    with ExitStack() as ctx:
        const = ctx.enter_context(tc.tile_pool(name="const", bufs=1))
        xin = ctx.enter_context(tc.tile_pool(name="xin", bufs=3))
        win = ctx.enter_context(tc.tile_pool(name="win", bufs=2))
        xcol = ctx.enter_context(tc.tile_pool(name="xcol", bufs=5))
        work = ctx.enter_context(tc.tile_pool(name="work", bufs=3))
        mid = ctx.enter_context(tc.tile_pool(name="mid", bufs=2))
        wq = ctx.enter_context(tc.tile_pool(name="wq", bufs=3))
        xq = ctx.enter_context(tc.tile_pool(name="xq", bufs=6))
        st0 = ctx.enter_context(tc.tile_pool(name="st0", bufs=3))
        st1 = ctx.enter_context(tc.tile_pool(name="st1", bufs=5))
        acc_pool = ctx.enter_context(tc.psum_pool(name="acc", bufs=5))
        tr_pool = ctx.enter_context(tc.psum_pool(name="tr", bufs=3))
        ctx.enter_context(tc.manual_schedule())

        pos = const.tile([P, HID], BF16, name="pos")
        nc.sync.dma_start(out=pos[0:TOKENS, :], in_=pos_embed[1 : 1 + TOKENS, :])
        grad = work.tile([P, GRID, HID], BF16, name="grad", tag="work", align_bytes=64)
        for gy in range(GRID):
            (nc.scalar if gy % 2 else nc.sync).dma_start(
                out=grad[:, gy, :], in_=grad_out[:, 1 + GRID * gy : 1 + GRID * (gy + 1), :]
            )
        w_rows = W.rearrange("(p j) w -> p j w", j=PACK)
        w_raw, x_raw = [], []
        for c in range(CHANNELS):
            w_tile = win.tile([P, PACK, PATCH * PATCH], BF16, name="w_tile", align_bytes=64)
            nc.sync.dma_start(
                out=w_tile[:], in_=w_rows[:, :, c * PATCH * PATCH : (c + 1) * PATCH * PATCH]
            )
            w_raw.append(w_tile)
            x_tile = xin.tile([P, IMAGES, 2 * SIDE], BF16, name="x_tile", align_bytes=64)
            nc.sync.dma_start(
                out=x_tile[:], in_=X[:, c, :, :].rearrange("n (y l) x -> y n (l x)", l=2)
            )
            x_raw.append(x_tile)

        ident = const.tile([P, P], BF16, name="ident")
        make_identity(nc, ident[:])
        ident_f = const.tile([P, P], F32, name="ident_f")
        make_identity(nc, ident_f[:])
        nc.vector.memset(pos[TOKENS:P, :], 0.0)
        spread = const.tile([P, GRID, IMAGES, GRID], BF16, name="spread")
        nc.vector.tensor_copy(
            out=spread[:],
            in_=ident[:, 0:TOKENS]
            .rearrange("p (y x) -> p y x", x=GRID)
            .unsqueeze(2)
            .to_broadcast([P, GRID, IMAGES, GRID]),
        )
        perm_x = const.tile([P, 2, PATCH // 2, PACK], BF16, name="perm_x")
        nc.vector.tensor_copy(
            out=perm_x[:], in_=ident[:].rearrange("p (g t y) -> p g y t", g=2, t=PACK)
        )

        dz = work.tile([P, GRID, HID], BF16, name="dz", tag="work", align_bytes=64)
        for a in range(GRID // 2):
            bank = tr_pool.tile([P, 2, HID], BF16, name="pos_bank", tag="tr")
            for e in range(2):
                nc.tensor.matmul(
                    out=bank[:, e, :],
                    lhsT=spread[:, 2 * a + e, :, :].rearrange("p n x -> p (n x)"),
                    rhs=pos[:],
                    start=True,
                    stop=True,
                )
            for e in range(2):
                gy = 2 * a + e
                nc.vector.tensor_tensor(
                    out=dz[:, gy, :], in0=grad[:, gy, :], in1=bank[:, e, :], op=mybir.AluOpType.mult
                )

        def weight_grouped(k, q, t, engine):
            src = w_raw[k // 2][:, :, (k % 2) * N_TILE + q * 256 : (k % 2) * N_TILE + (q + 1) * 256]
            engine(
                out=t[:, q * 256 : (q + 1) * 256, :].rearrange("p (c i) j -> p c j i", i=4),
                in_=src.rearrange("p j (c i) -> p c j i", i=4),
            )

        def weight_tile():
            return mid.tile([P, N_TILE, PACK], BF16, name="w_group", align_bytes=64)

        def weight_quantized(t):
            codes = wq.tile([P, N_TILE], U32, name="w_codes", align_bytes=64)
            scales = wq.tile([P, N_TILE], U8, name="w_scales", align_bytes=64)
            nc.vector.quantize_mx(
                out=codes[:].bitcast(E4M3), scales=scales[:], in_=t[:].rearrange("p w j -> p (w j)")
            )
            return codes, scales

        dzt_codes = const.tile([P, 2, HID], U32, name="dzt_codes", align_bytes=64)
        dzt_scales = const.tile([P, 2, HID], U8, name="dzt_scales", align_bytes=64)

        def tokens_grouped(g, engine):
            t = mid.tile([P, HID, PACK], BF16, name="dzt", align_bytes=64)
            engine(
                out=t[:].rearrange("p (c i) t -> p c t i", i=4),
                in_=dz[:, PACK * g : PACK * (g + 1), :].rearrange("p t (c i) -> p c t i", i=4),
            )
            return t

        def tokens_quantized(g, t):
            nc.vector.quantize_mx(
                out=dzt_codes[:, g, :].bitcast(E5M2),
                scales=dzt_scales[:, g, :],
                in_=t[:].rearrange("p f t -> p (f t)"),
            )

        dzf = work.tile([P, 8 * P, PACK], BF16, name="dzf", tag="work", align_bytes=64)
        dzf_words = (
            dzf[:]
            .rearrange("p m t -> p (m t)")
            .bitcast(F32)
            .rearrange("p (x g n k) -> p x g n k", x=GRID, g=2, k=8)
        )
        for a in range(GRID // 2):
            bank = tr_pool.tile([P, 4, P], F32, name="dz_bank", tag="tr")
            for e in range(2):
                words = dz[:, 2 * a + e, :].bitcast(F32)
                for u in range(2):
                    nc.tensor.transpose(
                        bank[:, 2 * e + u, :], words[:, u : HID // 2 : 2], ident_f[:]
                    )
            src = bank[:].rearrange("p k (n x) -> p x n k", x=GRID)
            dst = dzf_words[:, :, a // 2, :, 4 * (a % 2) : 4 * (a % 2) + 4]
            if a % 2 == 0:
                nc.scalar.copy(out=dst, in_=src)
            else:
                nc.vector.tensor_copy(out=dst, in_=src)
        w_group = weight_tile()
        weight_grouped(0, 0, w_group, nc.scalar.copy)
        weight_grouped(0, 1, w_group, nc.scalar.copy)
        dzf_codes = const.tile([P, 8 * P], U32, name="dzf_codes", align_bytes=64)
        dzf_scales = const.tile([P, 8 * P], U8, name="dzf_scales", align_bytes=64)
        dzt_0 = tokens_grouped(0, nc.vector.tensor_copy)
        nc.vector.quantize_mx(
            out=dzf_codes[:].bitcast(E5M2),
            scales=dzf_scales[:],
            in_=dzf[:].rearrange("p m t -> p (m t)"),
        )
        tokens_quantized(0, dzt_0)
        w_next = weight_quantized(w_group)

        x_cols, x_banks, x_groups, x_codes = {}, {}, {}, {}

        def image_columns(i):
            unit, j = divmod(i, 4)
            c, l = divmod(unit, 2)
            t = xcol.tile([P, BANK_PX // 2, P, 2], BF16, name="x_col", align_bytes=64)
            words = t[:].rearrange("p w r e -> p (w r e)").bitcast(F32)
            raw = x_raw[c][:].rearrange("p n f -> p (n f)").bitcast(F32)
            for a in range(2):
                nc.vector.tensor_copy(
                    out=words.rearrange("p (a i n x) -> p a n x i", a=2, i=2, x=GRID)[:, a],
                    in_=raw.rearrange("p (n l x w i) -> p l w n x i", l=2, x=GRID, w=8, i=2)[
                        :, l, 2 * j + a
                    ],
                )
            x_cols[i] = t

        def image_transposes(i):
            bank = tr_pool.tile([P, 2, PATCH // 2, BANK_PX, PACK], BF16, name="x_bank", tag="tr")
            for e in range(BANK_PX):
                if i % 8 in (0, 1, 2, 4, 5):
                    nc.tensor.matmul(
                        out=bank[:, :, :, e, :],
                        lhsT=x_cols[i][:, e // 2, :, e % 2],
                        rhs=perm_x[:],
                        start=True,
                        stop=True,
                    )
                else:
                    nc.tensor.transpose(
                        bank[:, :, :, e, :], x_cols[i][:, e // 2, :, e % 2], perm_x[:]
                    )
            x_banks[i] = bank

        def image_grouped(i, engine):
            if i % 4 == 0:
                x_groups[i // 4] = work.tile(
                    [P, 2, 4, 16 * BANK_PX * PACK], BF16, name="x_group", tag="work", align_bytes=64
                )
            engine(
                out=x_groups[i // 4][:, :, i % 4, :],
                in_=x_banks[i][:].rearrange("p g y x t -> p g (y x t)"),
            )

        def image_quantized(i):
            codes = xq.tile([P, 2, N_TILE], U32, name="x_codes", align_bytes=64)
            scales = xq.tile([P, 2, N_TILE], U8, name="x_scales", align_bytes=64)
            nc.vector.quantize_mx(
                out=codes[:].rearrange("p g n -> p (g n)").bitcast(E4M3),
                scales=scales[:].rearrange("p g n -> p (g n)"),
                in_=x_groups[i][:].rearrange("p g j f -> p (g j f)"),
            )
            x_codes[i] = (codes, scales)

        def image_gradient(stage, w, gx, engine):
            acc = acc_pool.tile([P, N_TILE], F32, name="acc", tag="acc")
            cols = slice(gx * P, (gx + 1) * P)
            nc.tensor.matmul_mx(
                out=acc[:],
                lhsT=dzf_codes[:, cols].bitcast(E5M2),
                lhsT_scale=dzf_scales[:, cols],
                rhs=w[0][:].bitcast(E4M3),
                rhs_scale=w[1][:],
                start=True,
                stop=True,
            )
            engine(out=stage[:, :, gx, :], in_=acc[:].rearrange("p (y x) -> p y x", x=PATCH))

        stages = {}

        def weight_gradient(c, m, h):
            codes, scales = x_codes[2 * c + h]
            if h == 0:
                stages[c, m] = st1.tile([P, PATCH // 2, 2, 4, BANK_PX], F32, name="stage1", align_bytes=64)
            acc = acc_pool.tile([P, N_TILE], F32, name="acc1", tag="acc")
            for g in range(2):
                nc.tensor.matmul_mx(
                    out=acc[:],
                    lhsT=dzt_codes[:, g, m * P : (m + 1) * P].bitcast(E5M2),
                    lhsT_scale=dzt_scales[:, g, m * P : (m + 1) * P],
                    rhs=codes[:, g, :].bitcast(E4M3),
                    rhs_scale=scales[:, g, :],
                    start=(g == 0),
                    stop=(g == 1),
                )
            return acc, c, m, h

        def weight_gradient_out(acc, c, m, h, engine):
            engine(
                out=stages[c, m][:, :, h, :, :].rearrange("p y j x -> p j y x"),
                in_=acc[:].rearrange("p (j y x) -> p j y x", j=4, x=BANK_PX),
            )
            if h == 1:
                nc.sync.dma_start(
                    out=out_1[m * P : (m + 1) * P, c * PATCH * PATCH : (c + 1) * PATCH * PATCH],
                    in_=stages[c, m][:].rearrange("p y l j x -> p (y l j x)"),
                )

        x_slot = [i * 6 // 5 for i in range(BANKS)]
        groups = [(x_slot[8 * c + 7] + 3, c, m, h) for c in range(CHANNELS) for m in range(4) for h in range(2)]
        v, a = nc.vector.tensor_copy, nc.scalar.copy
        for i in range(3):
            image_columns(i)
        ahead = 3
        ws = {0: w_next}
        w_groups = {}
        banks, quants, outs, stores = [], [], [], []
        dzt_1 = None
        count = 0

        def weight_group_step(s):
            kw, q = divmod(s + 4, 4)
            if 1 <= kw < CHUNKS and q < 2:
                if q == 0:
                    w_groups[kw] = weight_tile()
                weight_grouped(kw, q, w_groups[kw], v)

        def weight_quantize_step(s):
            kw, q = divmod(s + 4, 4)
            if 1 <= kw < CHUNKS and q == 2:
                ws[kw] = weight_quantized(w_groups[kw])

        for s in range(4 - 4, 0):
            weight_group_step(s)
            weight_quantize_step(s)
        s = 0
        while s < SLOTS or groups or outs or banks or quants or stores:
            k, r = divmod(s, 4)
            if s < SLOTS:
                if r == 0:
                    stage = st0.tile([P, PATCH // 2, GRID, PATCH], F32, name="stage0", align_bytes=64)
                for e in range(2):
                    image_gradient(stage, ws[k], 2 * r + e, a)
            for out_ap, in_ap in stores:
                nc.gpsimd.dma_start(out=out_ap, in_=in_ap)
            stores = []
            if s == 1:
                dzt_1 = tokens_grouped(1, v)
            if s == 1 + 1:
                tokens_quantized(1, dzt_1)
            weight_group_step(s)
            new_banks = []
            for i in range(BANKS):
                if x_slot[i] == s:
                    image_transposes(i)
                    new_banks.append(i)
                    if ahead < BANKS:
                        image_columns(ahead)
                        ahead += 1
            weight_quantize_step(s)
            new_quants = []
            for i in banks:
                image_grouped(i, v if i % 4 == 3 else a)
                if i % 4 == 3:
                    new_quants.append(i // 4)
            banks = new_banks
            for args in outs:
                weight_gradient_out(*args, a if args[1] == 2 and (args[2] + args[3]) % 2 else v)
                count += 1
            outs = []
            for n in range(3):
                if groups and groups[0][0] <= s and (n == 0 or s >= 20) and (s >= 8):
                    slot, c, m, h = groups.pop(0)
                    outs.append(weight_gradient(c, m, h))
            for i in quants:
                image_quantized(i)
            quants = new_quants
            if s < SLOTS and r == 3:
                y0 = (k % 2) * (PATCH // 2)
                for n0 in (0, IMAGES // 2):
                    for g in range(2):
                        stores.append(
                            (
                                out_0[n0 : n0 + 8, k // 2, g * P : (g + 1) * P, :].rearrange(
                                    "n (g y) x -> n g (y x)", g=PACK
                                )[:, :, y0 * SIDE : (y0 + PATCH // 2) * SIDE],
                                stage[64 * g + 4 * n0 : 64 * g + 4 * n0 + 32].rearrange(
                                    "p y g x -> p (y g x)"
                                ),
                            )
                        )
            s += 1
